import numpy as np
import ml_dtypes

BF16 = ml_dtypes.bfloat16


def bf(x):
    return np.asarray(x, np.float32).astype(BF16)


def f32(x):
    return np.asarray(x, np.float32)


def f64(x):
    return np.asarray(x).astype(np.float64)


def striped(idx):
    return np.tile(idx.reshape(-1, 16).T, (8, 1))


C, S, N = 128, 256, 128


def sigmoid(v):
    return 1.0 / (1.0 + np.exp(-v))


def setup_inputs():
    return {"base": f32(np.random.standard_normal((C, S))), "hcat": f32(bf(np.random.standard_normal((C, N)))), "w_gate": bf(np.random.standard_normal((C, C)) / np.sqrt(C)), "b_gate": f32(0.5 * np.random.standard_normal((C, 1))), "offs": striped(np.random.permutation(S)[:N])}


def reference(base, hcat, w_gate, b_gate, offs):
    idx = offs[:16].T.reshape(-1)
    h = f64(hcat)
    gate = sigmoid(f64(w_gate).T @ h + f64(b_gate))
    out = f64(base).copy()
    out[:, idx] = gate * h
    return out

@@ -1,0 +1,42 @@
+import concourse.mybir as mybir
+
+C = 128
+S = 256
+N = 128
+
+FLOPS = 2 * C * C * N
+
+F32 = mybir.dt.float32
+BF16 = mybir.dt.bfloat16
+U16 = mybir.dt.uint16
+
+
+def tile_linkpredictor_kernel(tc, base, hcat, w_gate, b_gate, offs, out):
+    nc = tc.nc
+    with (
+        tc.tile_pool(name="held", bufs=1) as held,
+        tc.psum_pool(name="psum", bufs=1) as psum,
+    ):
+        offsets = held.tile([C, N // 16], U16, name="offsets")
+        features = held.tile([C, N], F32, name="features")
+        weights = held.tile([C, C], BF16, name="weights")
+        bias = held.tile([C, 1], F32, name="bias")
+        store = held.tile([C, S], F32, name="store")
+        nc.sync.dma_start(features[:], hcat)
+        nc.sync.dma_start(weights[:], w_gate)
+        nc.sync.dma_start(bias[:], b_gate)
+        nc.sync.dma_start(offsets[:], offs)
+        nc.sync.dma_start(store[:], base)
+
+        features_bf = held.tile([C, N], BF16, name="features_bf")
+        nc.vector.tensor_copy(features_bf[:], features[:])
+
+        logits = psum.tile([C, N], F32, name="logits")
+        nc.tensor.matmul(logits[:], weights[:], features_bf[:], start=True, stop=True)
+
+        gate = held.tile([C, N], F32, name="gate")
+        nc.scalar.activation(gate[:], logits[:], mybir.ActivationFunctionType.Sigmoid, bias=bias[:])
+
+        nc.vector.tensor_tensor(store[:].indirect(offsets[:]), gate[:], features[:], mybir.AluOpType.mult)
+
+        nc.sync.dma_start(out, store[:])

@@ -22,6 +22,10 @@ def tile_linkpredictor_kernel(tc, base, hcat, w_gate, b_gate, offs, out):
         weights = held.tile([C, C], BF16, name="weights")
         bias = held.tile([C, 1], F32, name="bias")
         store = held.tile([C, S], F32, name="store")
+        scratch = held.tile([C, 1], F32, name="scratch")
+        nc.vector.memset(scratch[:], 0.0)
+        nc.scalar.activation(scratch[:], scratch[:], mybir.ActivationFunctionType.Sigmoid)
+
         nc.sync.dma_start(features[:], hcat)
         nc.sync.dma_start(weights[:], w_gate)
         nc.sync.dma_start(bias[:], b_gate)

@@ -32,11 +32,10 @@ def tile_linkpredictor_kernel(tc, base, hcat, w_gate, b_gate, offs, out):
         nc.sync.dma_start(offsets[:], offs)
         nc.sync.dma_start(store[:], base)
 
-        features_bf = held.tile([C, N], BF16, name="features_bf")
-        nc.vector.tensor_copy(features_bf[:], features[:])
+        features_bf = features[:].bitcast(BF16)[:, 1::2]
 
         logits = psum.tile([C, N], F32, name="logits")
-        nc.tensor.matmul(logits[:], weights[:], features_bf[:], start=True, stop=True)
+        nc.tensor.matmul(logits[:], weights[:], features_bf, start=True, stop=True)
 
         gate = held.tile([C, N], F32, name="gate")
         nc.scalar.activation(gate[:], logits[:], mybir.ActivationFunctionType.Sigmoid, bias=bias[:])

@@ -22,15 +22,15 @@ def tile_linkpredictor_kernel(tc, base, hcat, w_gate, b_gate, offs, out):
         weights = held.tile([C, C], BF16, name="weights")
         bias = held.tile([C, 1], F32, name="bias")
         store = held.tile([C, S], F32, name="store")
+        nc.sync.dma_start(features[:], hcat)
+        nc.scalar.dma_start(weights[:], w_gate)
+        nc.scalar.dma_start(bias[:], b_gate)
+        nc.sync.dma_start(offsets[:], offs)
+        nc.sync.dma_start(store[:], base)
+
         scratch = held.tile([C, 1], F32, name="scratch")
         nc.vector.memset(scratch[:], 0.0)
         nc.scalar.activation(scratch[:], scratch[:], mybir.ActivationFunctionType.Sigmoid)
-
-        nc.sync.dma_start(features[:], hcat)
-        nc.sync.dma_start(weights[:], w_gate)
-        nc.sync.dma_start(bias[:], b_gate)
-        nc.sync.dma_start(offsets[:], offs)
-        nc.sync.dma_start(store[:], base)
 
         features_bf = features[:].bitcast(BF16)[:, 1::2]
 

@@ -3,6 +3,7 @@ import concourse.mybir as mybir
 C = 128
 S = 256
 N = 128
+ROW_ALIGN = 256
 
 FLOPS = 2 * C * C * N
 
@@ -18,10 +19,10 @@ def tile_linkpredictor_kernel(tc, base, hcat, w_gate, b_gate, offs, out):
         tc.psum_pool(name="psum", bufs=1) as psum,
     ):
         offsets = held.tile([C, N // 16], U16, name="offsets")
-        features = held.tile([C, N], F32, name="features")
-        weights = held.tile([C, C], BF16, name="weights")
+        features = held.tile([C, N], F32, name="features", align_bytes=ROW_ALIGN)
+        weights = held.tile([C, C], BF16, name="weights", align_bytes=ROW_ALIGN)
         bias = held.tile([C, 1], F32, name="bias")
-        store = held.tile([C, S], F32, name="store")
+        store = held.tile([C, S], F32, name="store", align_bytes=ROW_ALIGN)
         nc.sync.dma_start(features[:], hcat)
         nc.scalar.dma_start(weights[:], w_gate)
         nc.scalar.dma_start(bias[:], b_gate)

@@ -30,8 +30,7 @@ def tile_linkpredictor_kernel(tc, base, hcat, w_gate, b_gate, offs, out):
         nc.sync.dma_start(store[:], base)
 
         scratch = held.tile([C, 1], F32, name="scratch")
-        nc.vector.memset(scratch[:], 0.0)
-        nc.scalar.activation(scratch[:], scratch[:], mybir.ActivationFunctionType.Sigmoid)
+        nc.scalar.activation(scratch[:], bias[:], mybir.ActivationFunctionType.Sigmoid)
 
         features_bf = features[:].bitcast(BF16)[:, 1::2]
 

@@ -3,6 +3,7 @@ import concourse.mybir as mybir
 C = 128
 S = 256
 N = 128
+HALF = N // 2
 ROW_ALIGN = 256
 
 FLOPS = 2 * C * C * N
@@ -23,8 +24,8 @@ def tile_linkpredictor_kernel(tc, base, hcat, w_gate, b_gate, offs, out):
         weights = held.tile([C, C], BF16, name="weights", align_bytes=ROW_ALIGN)
         bias = held.tile([C, 1], F32, name="bias")
         store = held.tile([C, S], F32, name="store", align_bytes=ROW_ALIGN)
-        nc.sync.dma_start(features[:], hcat)
-        nc.scalar.dma_start(weights[:], w_gate)
+        nc.sync.dma_start(weights[:], w_gate)
+        nc.scalar.dma_start(features[:], hcat)
         nc.scalar.dma_start(bias[:], b_gate)
         nc.sync.dma_start(offsets[:], offs)
         nc.sync.dma_start(store[:], base)
@@ -34,11 +35,12 @@ def tile_linkpredictor_kernel(tc, base, hcat, w_gate, b_gate, offs, out):
 
         features_bf = features[:].bitcast(BF16)[:, 1::2]
 
-        logits = psum.tile([C, N], F32, name="logits")
-        nc.tensor.matmul(logits[:], weights[:], features_bf, start=True, stop=True)
-
         gate = held.tile([C, N], F32, name="gate")
-        nc.scalar.activation(gate[:], logits[:], mybir.ActivationFunctionType.Sigmoid, bias=bias[:])
+        for half in range(2):
+            edges = slice(half * HALF, (half + 1) * HALF)
+            logits = psum.tile([C, HALF], F32, name=f"logits_{half}")
+            nc.tensor.matmul(logits[:], weights[:], features_bf[:, edges], start=True, stop=True)
+            nc.scalar.activation(gate[:, edges], logits[:], mybir.ActivationFunctionType.Sigmoid, bias=bias[:])
 
         nc.vector.tensor_tensor(store[:].indirect(offsets[:]), gate[:], features[:], mybir.AluOpType.mult)
 

@@ -24,8 +24,8 @@ def tile_linkpredictor_kernel(tc, base, hcat, w_gate, b_gate, offs, out):
         weights = held.tile([C, C], BF16, name="weights", align_bytes=ROW_ALIGN)
         bias = held.tile([C, 1], F32, name="bias")
         store = held.tile([C, S], F32, name="store", align_bytes=ROW_ALIGN)
-        nc.sync.dma_start(weights[:], w_gate)
-        nc.scalar.dma_start(features[:], hcat)
+        nc.sync.dma_start(features[:], hcat)
+        nc.scalar.dma_start(weights[:], w_gate)
         nc.scalar.dma_start(bias[:], b_gate)
         nc.sync.dma_start(offsets[:], offs)
         nc.sync.dma_start(store[:], base)

import concourse.mybir as mybir

C = 128
S = 256
N = 128
HALF = N // 2
ROW_ALIGN = 256

FLOPS = 2 * C * C * N

F32 = mybir.dt.float32
BF16 = mybir.dt.bfloat16
U16 = mybir.dt.uint16


def tile_linkpredictor_kernel(tc, base, hcat, w_gate, b_gate, offs, out):
    nc = tc.nc
    with (
        tc.tile_pool(name="held", bufs=1) as held,
        tc.psum_pool(name="psum", bufs=1) as psum,
    ):
        offsets = held.tile([C, N // 16], U16, name="offsets")
        features = held.tile([C, N], F32, name="features", align_bytes=ROW_ALIGN)
        weights = held.tile([C, C], BF16, name="weights", align_bytes=ROW_ALIGN)
        bias = held.tile([C, 1], F32, name="bias")
        store = held.tile([C, S], F32, name="store", align_bytes=ROW_ALIGN)
        nc.sync.dma_start(features[:], hcat)
        nc.scalar.dma_start(weights[:], w_gate)
        nc.scalar.dma_start(bias[:], b_gate)
        nc.sync.dma_start(offsets[:], offs)
        nc.sync.dma_start(store[:], base)

        scratch = held.tile([C, 1], F32, name="scratch")
        nc.scalar.activation(scratch[:], bias[:], mybir.ActivationFunctionType.Sigmoid)

        features_bf = features[:].bitcast(BF16)[:, 1::2]

        gate = held.tile([C, N], F32, name="gate")
        for half in range(2):
            edges = slice(half * HALF, (half + 1) * HALF)
            logits = psum.tile([C, HALF], F32, name=f"logits_{half}")
            nc.tensor.matmul(logits[:], weights[:], features_bf[:, edges], start=True, stop=True)
            nc.scalar.activation(gate[:, edges], logits[:], mybir.ActivationFunctionType.Sigmoid, bias=bias[:])

        nc.vector.tensor_tensor(store[:].indirect(offsets[:]), gate[:], features[:], mybir.AluOpType.mult)

        nc.sync.dma_start(out, store[:])
